import numpy as np
import ml_dtypes


def mxq(x, axis, fmt="e4m3"):
    dtype, down = {"e4m3": (ml_dtypes.float8_e4m3fn, 7), "e5m2": (ml_dtypes.float8_e5m2, 14)}[fmt]
    v = np.moveaxis(np.asarray(x, np.float32).astype(ml_dtypes.bfloat16).astype(np.float64), axis, -1)
    blocks = v.reshape(v.shape[:-1] + (-1, 32))
    amax = np.abs(blocks).max(-1, keepdims=True)
    byte = np.maximum(np.where(amax > 0, np.frexp(amax)[1] - 1 + 127, 0) - down, 1)
    scale = np.exp2(byte - 127.0)
    codes = (blocks / scale).astype(np.float32).astype(dtype).astype(np.float64)
    return np.moveaxis((codes * scale).reshape(v.shape), -1, axis)


WIDE = False


def mx_kscale(k):
    if not WIDE:
        return np.ones(k)
    levels = np.array([10, -10, 5, -5, 0])
    a = np.random.permutation(np.resize(levels, k // 512 * 4)).reshape(k // 512, 4)
    idx = np.arange(k)
    return np.exp2(a[idx // 512, idx % 128 // 32])


BF16 = ml_dtypes.bfloat16


def bf(x):
    return np.asarray(x, np.float32).astype(BF16)


def f64(x):
    return np.asarray(x).astype(np.float64)


E2M1 = np.array([0.0, 0.5, 1.0, 1.5, 2.0, 3.0, 4.0, 6.0, -0.0, -0.5, -1.0, -1.5, -2.0, -3.0, -4.0, -6.0])


def pack_weight(w, fmt):
    k, n = w.shape
    w = f64(bf(w)).reshape(k // 32, 32, n)
    amax = np.abs(w).max(1)
    if fmt == "e4m3":
        byte = np.frexp(amax)[1] - 1 + 127 - 7
    else:
        mant, ex = np.frexp(amax / 6.0)
        byte = np.where(mant > 0.5, ex, ex - 1) + 127
    byte = np.clip(np.where(amax > 0, byte, 1), 1, 254)
    scaled = (w * np.exp2(127.0 - byte)[:, None, :]).reshape(k, n).astype(np.float32)
    by_word = np.ascontiguousarray(scaled.reshape(k // 512, 128, 4, n).transpose(0, 1, 3, 2))
    if fmt == "e4m3":
        words = by_word.astype(ml_dtypes.float8_e4m3fn).view(np.uint8)
    else:
        c = by_word.astype(ml_dtypes.float4_e2m1fn).view(np.uint8) & 0xF
        words = c[..., 0::2] | (c[..., 1::2] << 4)
    return np.ascontiguousarray(words), np.ascontiguousarray(byte.astype(np.uint8).reshape(k // 512, 16, n))


def unpack_weight(words, scales, fmt):
    g, p, n, _ = words.shape
    if fmt == "e4m3":
        vals = np.ascontiguousarray(words).view(ml_dtypes.float8_e4m3fn).astype(np.float64)
    else:
        nib = np.empty((g, p, n, 4), np.uint8)
        nib[..., 0::2] = words & 0xF
        nib[..., 1::2] = words >> 4
        vals = E2M1[nib]
    vals = vals * np.repeat(np.exp2(scales.astype(np.float64) - 127.0), 8, axis=1)[..., None]
    return vals.transpose(0, 1, 3, 2).reshape(g * 512, n)


N, IN_DIM, HID, NUM_CLASSES, AVG_DEG = 2048, 512, 512, 512, 32


def setup_inputs():
    s = mx_kscale(IN_DIM)
    edges = np.random.uniform(size=(N, N)) < AVG_DEG / N
    A = bf(edges * (0.5 + np.random.uniform(size=(N, N))))
    x = bf(np.random.standard_normal((N, IN_DIM)) * 0.5 * s)
    W1_words, W1_scales = pack_weight(np.random.standard_normal((IN_DIM, HID)) * 4.0 / np.sqrt(IN_DIM) / s[:, None], "e4m3")
    b1 = bf(np.random.standard_normal(HID) * 0.1)
    return {"A": A,
            "x": x,
            "W1_words": W1_words,
            "W1_scales": W1_scales,
            "b1": b1}


def reference(A, x, W1_words, W1_scales, b1):
    A = f64(A)
    deg = A.sum(0) + 1.0
    dis = (1.0 / np.sqrt(deg))[:, None]
    h = mxq(f64(x), 1, "e4m3") @ unpack_weight(W1_words, W1_scales, "e4m3")
    m = dis * h
    agg = mxq(A, 0, "e4m3").T @ mxq(m, 0, "e4m3")
    return np.maximum(dis * agg + dis ** 2 * h + f64(b1), 0.0)

@@ -1,0 +1,274 @@
+import concourse.mybir as mybir
+from concourse.masks import make_identity
+
+F32 = mybir.dt.float32
+BF16 = mybir.dt.bfloat16
+I32 = mybir.dt.int32
+U32 = mybir.dt.uint32
+U8 = mybir.dt.uint8
+FP8X4 = mybir.dt.float8_e4m3fn_x4
+ALU = mybir.AluOpType
+ACT = mybir.ActivationFunctionType
+
+P = 128
+PACK = 4
+CHUNK = P * PACK
+NODES = 2048
+FEAT = 512
+CHUNKS = NODES // CHUNK
+PSUM_BANKS = 8
+VECTOR_COLS = 208
+MESSAGES_LAG = 1
+
+FLOPS = 2 * NODES * FEAT * FEAT + 2 * NODES * NODES * FEAT
+
+
+def side_by_side(dst, src):
+    return (
+        dst.rearrange("p (c i) t -> p c t i", i=4),
+        src.rearrange("p t (c i) -> p c t i", i=4),
+    )
+
+
+def tile_gcnnodeclassifiernetwork_pa_kernel(tc, A, x, W1_words, W1_scales, b1, out):
+    nc = tc.nc
+    with (
+        tc.tile_pool(name="keep", bufs=1) as keep,
+        tc.tile_pool(name="x_in", bufs=CHUNKS) as x_in,
+        tc.tile_pool(name="x_grouped", bufs=2) as x_grouped,
+        tc.tile_pool(name="a_in", bufs=CHUNKS * CHUNKS) as a_in,
+        tc.tile_pool(name="a_grouped", bufs=3) as a_grouped,
+        tc.tile_pool(name="m_stage", bufs=2) as m_stage,
+        tc.tile_pool(name="degrees", bufs=CHUNKS) as degrees,
+        tc.tile_pool(name="result", bufs=6) as result,
+        tc.psum_pool(name="psum", bufs=PSUM_BANKS) as psum,
+        tc.manual_schedule(),
+    ):
+        w_scales = keep.tile([P, FEAT], U8, align_bytes=64)
+        nc.vector.memset(w_scales[:].bitcast(I32), 0)
+        for quad in range(4):
+            nc.sync.dma_start(
+                out=w_scales[32 * quad : 32 * quad + 4, :].bitcast(I32),
+                in_=W1_scales[0, 4 * quad : 4 * quad + 4, :].bitcast(I32),
+            )
+        w_codes = keep.tile([P, FEAT], U32, align_bytes=64)
+        nc.sync.dma_start(
+            out=w_codes[:].bitcast(I32),
+            in_=W1_words[0].rearrange("p n t -> p (n t)").bitcast(I32),
+        )
+        bias_row = keep.tile([P, FEAT], BF16)
+        nc.vector.memset(bias_row[:], 0.0)
+        nc.scalar.dma_start(out=bias_row[0:1, :], in_=b1.unsqueeze(0))
+
+        x_rows = {}
+        a_piece = {}
+
+        def load_x(c):
+            x_rows[c] = x_in.tile([P, PACK, FEAT], BF16, name="x_rows")
+            nc.sync.dma_start(
+                out=x_rows[c][:],
+                in_=x[CHUNK * c : CHUNK * (c + 1), :].rearrange("(t p) k -> p t k", p=P),
+            )
+
+        def load_a(q):
+            for c in range(CHUNKS):
+                a_piece[q, c] = a_in.tile([P, PACK, CHUNK], BF16, name="a_piece")
+                nc.sync.dma_start(
+                    out=a_piece[q, c][:],
+                    in_=A[CHUNK * c : CHUNK * (c + 1), CHUNK * q : CHUNK * (q + 1)].rearrange(
+                        "(t p) j -> p t j", p=P
+                    ),
+                )
+
+        load_x(0)
+        for q in range(CHUNKS):
+            if q + 1 < CHUNKS:
+                load_x(q + 1)
+            load_a(q)
+
+        ident = keep.tile([P, P], F32)
+        make_identity(nc, ident[:])
+        ones = keep.tile([P, P], BF16)
+        nc.vector.memset(ones[:], 1.0)
+        bias_ps = psum.tile([P, FEAT], F32, tag="bank")
+        nc.tensor.matmul(out=bias_ps[:], lhsT=ones[:], rhs=bias_row[:], start=True, stop=True)
+        bias = keep.tile([P, FEAT], F32)
+        nc.scalar.copy(out=bias[:], in_=bias_ps[:])
+
+        x_codes = keep.tile([P, NODES], U32, align_bytes=64)
+        x_scales = keep.tile([P, NODES], U8, align_bytes=64)
+        a_codes = keep.tile([P, CHUNKS, NODES], U32, align_bytes=64)
+        a_scales = keep.tile([P, CHUNKS, NODES], U8, align_bytes=64)
+        m_codes = keep.tile([P, CHUNKS, FEAT], U32, align_bytes=64)
+        m_scales = keep.tile([P, CHUNKS, FEAT], U8, align_bytes=64)
+        self_loop = keep.tile([P, CHUNKS * PACK, FEAT], F32)
+        d_of_chunk = {}
+        a_waiting = []
+
+        def quantise_x(c):
+            words = x_rows[c][:].rearrange("p t k -> p (t k)").bitcast(F32)
+            grouped = x_grouped.tile([P, PACK * P * PACK], BF16, align_bytes=64, name="x_side")
+            grouped_words = grouped[:].bitcast(F32).rearrange("p (t r u) -> p t r u", t=PACK, u=2)
+            for half in range(2):
+                flipped = psum.tile([P, 2, 2, P], F32, tag="bank")
+                for a in range(2):
+                    first = (FEAT // 2) * (2 * half + a)
+                    for u in range(2):
+                        nc.tensor.transpose(
+                            out=flipped[:, a, u, :],
+                            in_=words[:, first + u : first + FEAT // 2 : 2],
+                            identity=ident[:],
+                        )
+                nc.scalar.copy(
+                    out=grouped_words[:, 2 * half : 2 * half + 2, :, :],
+                    in_=flipped[:].rearrange("p a u r -> p a r u"),
+                )
+            cols = slice(CHUNK * c, CHUNK * (c + 1))
+            nc.vector.quantize_mx(
+                out=x_codes[:, cols].bitcast(FP8X4), scales=x_scales[:, cols], in_=grouped[:]
+            )
+
+        def column_sums(q, c, sums_ps):
+            for b in range(PACK):
+                for t in range(PACK):
+                    nc.tensor.matmul(
+                        out=sums_ps[:, b, c : c + 1],
+                        lhsT=a_piece[q, c][:, t, P * b : P * (b + 1)],
+                        rhs=ones[:, 0:1],
+                        start=(t == 0),
+                        stop=(t == PACK - 1),
+                    )
+
+        def quantise_waiting():
+            q, c, grouped = a_waiting.pop(0)
+            cols = slice(CHUNK * q, CHUNK * (q + 1))
+            nc.vector.quantize_mx(
+                out=a_codes[:, c, cols].bitcast(FP8X4),
+                scales=a_scales[:, c, cols],
+                in_=grouped[:].rearrange("p j t -> p (j t)"),
+            )
+
+        def quantise_a(q, c):
+            piece = a_piece[q, c]
+            grouped = a_grouped.tile([P, CHUNK, PACK], BF16, align_bytes=64, name="a_side")
+            dst, src = side_by_side(grouped[:, :VECTOR_COLS, :], piece[:, :, :VECTOR_COLS])
+            nc.vector.tensor_copy(out=dst, in_=src)
+            dst, src = side_by_side(grouped[:, VECTOR_COLS:, :], piece[:, :, VECTOR_COLS:])
+            nc.scalar.copy(out=dst, in_=src)
+            if a_waiting:
+                quantise_waiting()
+            a_waiting.append((q, c, grouped))
+
+        def hidden(c):
+            h_ps = []
+            for t in range(PACK):
+                cols = slice(CHUNK * c + P * t, CHUNK * c + P * (t + 1))
+                h_ps.append(psum.tile([P, FEAT], F32, tag="bank", name="h_ps"))
+                nc.tensor.matmul_mx(
+                    out=h_ps[t][:],
+                    lhsT=x_codes[:, cols].bitcast(FP8X4),
+                    lhsT_scale=x_scales[:, cols],
+                    rhs=w_codes[:].bitcast(FP8X4),
+                    rhs_scale=w_scales[:],
+                    start=True,
+                    stop=True,
+                )
+            return h_ps
+
+        def normalisers(sums_ps):
+            total = degrees.tile([P, PACK], F32)
+            nc.vector.tensor_reduce(out=total[:], in_=sums_ps[:], axis=mybir.AxisListType.X, op=ALU.add)
+            root = degrees.tile([P, PACK], F32)
+            nc.scalar.activation(out=root[:], in_=total[:], func=ACT.Sqrt, bias=1.0, scale=1.0)
+            d = degrees.tile([P, PACK], F32)
+            nc.vector.reciprocal(out=d[:], in_=root[:])
+            d_squared = degrees.tile([P, PACK], F32)
+            nc.vector.tensor_mul(out=d_squared[:], in0=d[:], in1=d[:])
+            return d, d_squared
+
+        def messages(c, h_ps, d, d_squared):
+            scaled = m_stage.tile([P, PACK, FEAT], BF16)
+            for t in range(PACK):
+                nc.scalar.activation(
+                    out=scaled[:, t, :], in_=h_ps[t][:], func=ACT.Copy, scale=d[:, t : t + 1]
+                )
+                nc.vector.scalar_tensor_tensor(
+                    out=self_loop[:, PACK * c + t, :],
+                    in0=h_ps[t][:],
+                    scalar=d_squared[:, t : t + 1],
+                    in1=bias[:],
+                    op0=ALU.mult,
+                    op1=ALU.add,
+                )
+            grouped = m_stage.tile([P, FEAT, PACK], BF16, align_bytes=64, name="m_side")
+            dst, src = side_by_side(grouped[:], scaled[:])
+            nc.vector.tensor_copy(out=dst, in_=src)
+            nc.vector.quantize_mx(
+                out=m_codes[:, c, :].bitcast(FP8X4),
+                scales=m_scales[:, c, :],
+                in_=grouped[:].rearrange("p n t -> p (n t)"),
+            )
+
+        last = CHUNKS - 1
+        sums_ps = {}
+        h_ps = {}
+
+        def messages_of(q):
+            d_of_chunk[q], d_squared = normalisers(sums_ps[q])
+            messages(q, h_ps[q], d_of_chunk[q], d_squared)
+
+        quantise_x(0)
+        for q in range(CHUNKS):
+            sums_ps[q] = psum.tile([P, PACK, CHUNKS], F32, tag="bank", name="sums_ps")
+            for c in range(CHUNKS):
+                if c == 0 and q < last:
+                    quantise_x(q + 1)
+                column_sums(q, c, sums_ps[q])
+                if q < last:
+                    quantise_a(q, c)
+                if c == MESSAGES_LAG and q > 0:
+                    messages_of(q - 1)
+            h_ps[q] = hidden(q)
+        messages_of(last)
+
+        agg_ps = {}
+
+        def passes(b, which):
+            cols = slice(P * b, P * (b + 1))
+            for c in which:
+                if c == 0:
+                    agg_ps[b] = psum.tile([P, FEAT], F32, tag="bank", name="agg_ps")
+                nc.tensor.matmul_mx(
+                    out=agg_ps[b][:],
+                    lhsT=a_codes[:, c, cols].bitcast(FP8X4),
+                    lhsT_scale=a_scales[:, c, cols],
+                    rhs=m_codes[:, c, :].bitcast(FP8X4),
+                    rhs_scale=m_scales[:, c, :],
+                    start=(c == 0),
+                    stop=(c == last),
+                )
+
+        def finish(b):
+            rows = result.tile([P, FEAT], F32)
+            nc.vector.scalar_tensor_tensor(
+                out=rows[:],
+                in0=agg_ps[b][:],
+                scalar=d_of_chunk[b // PACK][:, b % PACK : b % PACK + 1],
+                in1=self_loop[:, b, :],
+                op0=ALU.mult,
+                op1=ALU.add,
+            )
+            nc.scalar.activation(out=rows[:], in_=rows[:], func=ACT.Relu)
+            nc.sync.dma_start(out=out[P * b : P * (b + 1), :], in_=rows[:])
+
+        for b in range(PSUM_BANKS):
+            passes(b, range(last))
+        for b in range(PSUM_BANKS):
+            if b % 2 == 0:
+                quantise_a(last, b // 2)
+            passes(b, [last])
+            finish(b)
+        quantise_waiting()
+        for b in range(PSUM_BANKS, CHUNKS * PACK):
+            passes(b, range(CHUNKS))
+            finish(b)

@@ -17,8 +17,7 @@ NODES = 2048
 FEAT = 512
 CHUNKS = NODES // CHUNK
 PSUM_BANKS = 8
-VECTOR_COLS = 208
-MESSAGES_LAG = 1
+VECTOR_COLS = 240
 
 FLOPS = 2 * NODES * FEAT * FEAT + 2 * NODES * NODES * FEAT
 
@@ -36,11 +35,11 @@ def tile_gcnnodeclassifiernetwork_pa_kernel(tc, A, x, W1_words, W1_scales, b1, o
         tc.tile_pool(name="keep", bufs=1) as keep,
         tc.tile_pool(name="x_in", bufs=CHUNKS) as x_in,
         tc.tile_pool(name="x_grouped", bufs=2) as x_grouped,
-        tc.tile_pool(name="a_in", bufs=CHUNKS * CHUNKS) as a_in,
-        tc.tile_pool(name="a_grouped", bufs=3) as a_grouped,
+        tc.tile_pool(name="a_in", bufs=12) as a_in,
+        tc.tile_pool(name="a_grouped", bufs=4) as a_grouped,
         tc.tile_pool(name="m_stage", bufs=2) as m_stage,
         tc.tile_pool(name="degrees", bufs=CHUNKS) as degrees,
-        tc.tile_pool(name="result", bufs=6) as result,
+        tc.tile_pool(name="result", bufs=10) as result,
         tc.psum_pool(name="psum", bufs=PSUM_BANKS) as psum,
         tc.manual_schedule(),
     ):
@@ -128,16 +127,19 @@ def tile_gcnnodeclassifiernetwork_pa_kernel(tc, A, x, W1_words, W1_scales, b1, o
                 out=x_codes[:, cols].bitcast(FP8X4), scales=x_scales[:, cols], in_=grouped[:]
             )
 
-        def column_sums(q, c, sums_ps):
+        def column_sums(q):
+            sums_ps = psum.tile([P, PACK], F32, tag="bank")
             for b in range(PACK):
-                for t in range(PACK):
-                    nc.tensor.matmul(
-                        out=sums_ps[:, b, c : c + 1],
-                        lhsT=a_piece[q, c][:, t, P * b : P * (b + 1)],
-                        rhs=ones[:, 0:1],
-                        start=(t == 0),
-                        stop=(t == PACK - 1),
-                    )
+                for c in range(CHUNKS):
+                    for t in range(PACK):
+                        nc.tensor.matmul(
+                            out=sums_ps[:, b : b + 1],
+                            lhsT=a_piece[q, c][:, t, P * b : P * (b + 1)],
+                            rhs=ones[:, 0:1],
+                            start=(c == 0 and t == 0),
+                            stop=(c == CHUNKS - 1 and t == PACK - 1),
+                        )
+            return sums_ps
 
         def quantise_waiting():
             q, c, grouped = a_waiting.pop(0)
@@ -148,12 +150,13 @@ def tile_gcnnodeclassifiernetwork_pa_kernel(tc, A, x, W1_words, W1_scales, b1, o
                 in_=grouped[:].rearrange("p j t -> p (j t)"),
             )
 
-        def quantise_a(q, c):
+        def quantise_a(q, c, vector_cols):
             piece = a_piece[q, c]
             grouped = a_grouped.tile([P, CHUNK, PACK], BF16, align_bytes=64, name="a_side")
-            dst, src = side_by_side(grouped[:, :VECTOR_COLS, :], piece[:, :, :VECTOR_COLS])
-            nc.vector.tensor_copy(out=dst, in_=src)
-            dst, src = side_by_side(grouped[:, VECTOR_COLS:, :], piece[:, :, VECTOR_COLS:])
+            if vector_cols:
+                dst, src = side_by_side(grouped[:, :vector_cols, :], piece[:, :, :vector_cols])
+                nc.vector.tensor_copy(out=dst, in_=src)
+            dst, src = side_by_side(grouped[:, vector_cols:, :], piece[:, :, vector_cols:])
             nc.scalar.copy(out=dst, in_=src)
             if a_waiting:
                 quantise_waiting()
@@ -176,14 +179,12 @@ def tile_gcnnodeclassifiernetwork_pa_kernel(tc, A, x, W1_words, W1_scales, b1, o
             return h_ps
 
         def normalisers(sums_ps):
-            total = degrees.tile([P, PACK], F32)
-            nc.vector.tensor_reduce(out=total[:], in_=sums_ps[:], axis=mybir.AxisListType.X, op=ALU.add)
-            root = degrees.tile([P, PACK], F32)
-            nc.scalar.activation(out=root[:], in_=total[:], func=ACT.Sqrt, bias=1.0, scale=1.0)
             d = degrees.tile([P, PACK], F32)
-            nc.vector.reciprocal(out=d[:], in_=root[:])
+            nc.scalar.activation(
+                out=d[:], in_=sums_ps[:], func=ACT.Abs_reciprocal_sqrt, bias=1.0, scale=1.0
+            )
             d_squared = degrees.tile([P, PACK], F32)
-            nc.vector.tensor_mul(out=d_squared[:], in0=d[:], in1=d[:])
+            nc.scalar.activation(out=d_squared[:], in_=d[:], func=ACT.Square)
             return d, d_squared
 
         def messages(c, h_ps, d, d_squared):
@@ -192,10 +193,11 @@ def tile_gcnnodeclassifiernetwork_pa_kernel(tc, A, x, W1_words, W1_scales, b1, o
                 nc.scalar.activation(
                     out=scaled[:, t, :], in_=h_ps[t][:], func=ACT.Copy, scale=d[:, t : t + 1]
                 )
+                v = PACK - 1 - t
                 nc.vector.scalar_tensor_tensor(
-                    out=self_loop[:, PACK * c + t, :],
-                    in0=h_ps[t][:],
-                    scalar=d_squared[:, t : t + 1],
+                    out=self_loop[:, PACK * c + v, :],
+                    in0=h_ps[v][:],
+                    scalar=d_squared[:, v : v + 1],
                     in1=bias[:],
                     op0=ALU.mult,
                     op1=ALU.add,
@@ -210,26 +212,18 @@ def tile_gcnnodeclassifiernetwork_pa_kernel(tc, A, x, W1_words, W1_scales, b1, o
             )
 
         last = CHUNKS - 1
-        sums_ps = {}
-        h_ps = {}
-
-        def messages_of(q):
-            d_of_chunk[q], d_squared = normalisers(sums_ps[q])
-            messages(q, h_ps[q], d_of_chunk[q], d_squared)
-
         quantise_x(0)
         for q in range(CHUNKS):
-            sums_ps[q] = psum.tile([P, PACK, CHUNKS], F32, tag="bank", name="sums_ps")
-            for c in range(CHUNKS):
-                if c == 0 and q < last:
-                    quantise_x(q + 1)
-                column_sums(q, c, sums_ps[q])
-                if q < last:
-                    quantise_a(q, c)
-                if c == MESSAGES_LAG and q > 0:
-                    messages_of(q - 1)
-            h_ps[q] = hidden(q)
-        messages_of(last)
+            if q < last:
+                quantise_x(q + 1)
+                for c in range(CHUNKS):
+                    quantise_a(q, c, VECTOR_COLS)
+            sums_ps = column_sums(q)
+            h_ps = hidden(q)
+            d_of_chunk[q], d_squared = normalisers(sums_ps)
+            messages(q, h_ps, d_of_chunk[q], d_squared)
+        for c in range(CHUNKS):
+            quantise_a(last, c, 0)
 
         agg_ps = {}
 
@@ -264,8 +258,6 @@ def tile_gcnnodeclassifiernetwork_pa_kernel(tc, A, x, W1_words, W1_scales, b1, o
         for b in range(PSUM_BANKS):
             passes(b, range(last))
         for b in range(PSUM_BANKS):
-            if b % 2 == 0:
-                quantise_a(last, b // 2)
             passes(b, [last])
             finish(b)
         quantise_waiting()

@@ -85,6 +85,9 @@ def tile_gcnnodeclassifiernetwork_pa_kernel(tc, A, x, W1_words, W1_scales, b1, o
                 load_x(q + 1)
             load_a(q)
 
+        warm = keep.tile([P, 1], F32)
+        nc.vector.memset(warm[:], 1.0)
+        nc.scalar.activation(out=warm[:], in_=warm[:], func=ACT.Abs_reciprocal_sqrt)
         ident = keep.tile([P, P], F32)
         make_identity(nc, ident[:])
         ones = keep.tile([P, P], BF16)
@@ -252,7 +255,9 @@ def tile_gcnnodeclassifiernetwork_pa_kernel(tc, A, x, W1_words, W1_scales, b1, o
                 op0=ALU.mult,
                 op1=ALU.add,
             )
-            nc.scalar.activation(out=rows[:], in_=rows[:], func=ACT.Relu)
+            nc.gpsimd.tensor_scalar(
+                out=rows[:], in0=rows[:], scalar1=0.0, scalar2=0.0, op0=ALU.max, op1=ALU.add
+            )
             nc.sync.dma_start(out=out[P * b : P * (b + 1), :], in_=rows[:])
 
         for b in range(PSUM_BANKS):

@@ -43,22 +43,6 @@ def tile_gcnnodeclassifiernetwork_pa_kernel(tc, A, x, W1_words, W1_scales, b1, o
         tc.psum_pool(name="psum", bufs=PSUM_BANKS) as psum,
         tc.manual_schedule(),
     ):
-        w_scales = keep.tile([P, FEAT], U8, align_bytes=64)
-        nc.vector.memset(w_scales[:].bitcast(I32), 0)
-        for quad in range(4):
-            nc.sync.dma_start(
-                out=w_scales[32 * quad : 32 * quad + 4, :].bitcast(I32),
-                in_=W1_scales[0, 4 * quad : 4 * quad + 4, :].bitcast(I32),
-            )
-        w_codes = keep.tile([P, FEAT], U32, align_bytes=64)
-        nc.sync.dma_start(
-            out=w_codes[:].bitcast(I32),
-            in_=W1_words[0].rearrange("p n t -> p (n t)").bitcast(I32),
-        )
-        bias_row = keep.tile([P, FEAT], BF16)
-        nc.vector.memset(bias_row[:], 0.0)
-        nc.scalar.dma_start(out=bias_row[0:1, :], in_=b1.unsqueeze(0))
-
         x_rows = {}
         a_piece = {}
 
@@ -79,11 +63,31 @@ def tile_gcnnodeclassifiernetwork_pa_kernel(tc, A, x, W1_words, W1_scales, b1, o
                     ),
                 )
 
+        w_scales = keep.tile([P, FEAT], U8, align_bytes=64)
+        w_codes = keep.tile([P, FEAT], U32, align_bytes=64)
+        nc.vector.memset(w_scales[:].bitcast(I32), 0)
+        bias_row = keep.tile([P, FEAT], BF16)
+        nc.vector.memset(bias_row[:], 0.0)
+        nc.scalar.dma_start(out=bias_row[0:1, :], in_=b1.unsqueeze(0))
+
+        def load_w():
+            for quad in range(4):
+                nc.sync.dma_start(
+                    out=w_scales[32 * quad : 32 * quad + 4, :].bitcast(I32),
+                    in_=W1_scales[0, 4 * quad : 4 * quad + 4, :].bitcast(I32),
+                )
+            nc.sync.dma_start(
+                out=w_codes[:].bitcast(I32),
+                in_=W1_words[0].rearrange("p n t -> p (n t)").bitcast(I32),
+            )
+
         load_x(0)
         for q in range(CHUNKS):
             if q + 1 < CHUNKS:
                 load_x(q + 1)
             load_a(q)
+            if q == 0:
+                load_w()
 
         warm = keep.tile([P, 1], F32)
         nc.vector.memset(warm[:], 1.0)
@@ -255,9 +259,7 @@ def tile_gcnnodeclassifiernetwork_pa_kernel(tc, A, x, W1_words, W1_scales, b1, o
                 op0=ALU.mult,
                 op1=ALU.add,
             )
-            nc.gpsimd.tensor_scalar(
-                out=rows[:], in0=rows[:], scalar1=0.0, scalar2=0.0, op0=ALU.max, op1=ALU.add
-            )
+            nc.scalar.activation(out=rows[:], in_=rows[:], func=ACT.Relu)
             nc.sync.dma_start(out=out[P * b : P * (b + 1), :], in_=rows[:])
 
         for b in range(PSUM_BANKS):

@@ -200,11 +200,10 @@ def tile_gcnnodeclassifiernetwork_pa_kernel(tc, A, x, W1_words, W1_scales, b1, o
                 nc.scalar.activation(
                     out=scaled[:, t, :], in_=h_ps[t][:], func=ACT.Copy, scale=d[:, t : t + 1]
                 )
-                v = PACK - 1 - t
                 nc.vector.scalar_tensor_tensor(
-                    out=self_loop[:, PACK * c + v, :],
-                    in0=h_ps[v][:],
-                    scalar=d_squared[:, v : v + 1],
+                    out=self_loop[:, PACK * c + t, :],
+                    in0=h_ps[t][:],
+                    scalar=d_squared[:, t : t + 1],
                     in1=bias[:],
                     op0=ALU.mult,
                     op1=ALU.add,

@@ -16,8 +16,18 @@ CHUNK = P * PACK
 NODES = 2048
 FEAT = 512
 CHUNKS = NODES // CHUNK
-PSUM_BANKS = 8
-VECTOR_COLS = 240
+BLOCKS = NODES // P
+LAST = CHUNKS - 1
+HIDDEN_BANKS = (0, 1, 2, 3)
+SUMS_BANK = 4
+SCRATCH_BANKS = (5, 6, 7)
+AGG_BANKS = (5, 6, 7, 4, 0, 1, 2, 3)
+PIECES_BEFORE_M = (4, 3, 2, 1)
+VECTOR_COLS = (240, 208, 208, 208, 128)
+UP = 3
+SPREAD = 8
+EXTRA = 2
+X_AT = (1, 0, 0, 0)
 
 FLOPS = 2 * NODES * FEAT * FEAT + 2 * NODES * NODES * FEAT
 
@@ -33,41 +43,52 @@ def tile_gcnnodeclassifiernetwork_pa_kernel(tc, A, x, W1_words, W1_scales, b1, o
     nc = tc.nc
     with (
         tc.tile_pool(name="keep", bufs=1) as keep,
-        tc.tile_pool(name="x_in", bufs=CHUNKS) as x_in,
+        tc.tile_pool(name="raw", bufs=16) as raw,
         tc.tile_pool(name="x_grouped", bufs=2) as x_grouped,
-        tc.tile_pool(name="a_in", bufs=12) as a_in,
-        tc.tile_pool(name="a_grouped", bufs=4) as a_grouped,
+        tc.tile_pool(name="a_grouped", bufs=6) as a_grouped,
         tc.tile_pool(name="m_stage", bufs=2) as m_stage,
         tc.tile_pool(name="degrees", bufs=CHUNKS) as degrees,
-        tc.tile_pool(name="result", bufs=10) as result,
-        tc.psum_pool(name="psum", bufs=PSUM_BANKS) as psum,
+        tc.tile_pool(name="result", bufs=8) as result,
+        tc.psum_pool(name="psum", bufs=1) as psum,
         tc.manual_schedule(),
     ):
+
+        def bank(i, shape, dtype=F32):
+            return psum.tile(shape, dtype, tag="bank%d" % i, name="bank")
+
+        scratch_banks = list(SCRATCH_BANKS)
+
+        def scratch_bank(shape, dtype=F32):
+            scratch_banks.append(scratch_banks.pop(0))
+            return bank(scratch_banks[-1], shape, dtype)
+
         x_rows = {}
         a_piece = {}
 
-        def load_x(c):
-            x_rows[c] = x_in.tile([P, PACK, FEAT], BF16, name="x_rows")
-            nc.sync.dma_start(
-                out=x_rows[c][:],
-                in_=x[CHUNK * c : CHUNK * (c + 1), :].rearrange("(t p) k -> p t k", p=P),
-            )
-
-        def load_a(q):
-            for c in range(CHUNKS):
-                a_piece[q, c] = a_in.tile([P, PACK, CHUNK], BF16, name="a_piece")
+        def load_x(c, parts):
+            x_rows[c] = raw.tile([P, PACK, FEAT], BF16, name="raw_rows")
+            rows = x[CHUNK * c : CHUNK * (c + 1), :].rearrange("(t p) k -> p t k", p=P)
+            size = PACK // parts
+            for i in range(parts):
                 nc.sync.dma_start(
-                    out=a_piece[q, c][:],
-                    in_=A[CHUNK * c : CHUNK * (c + 1), CHUNK * q : CHUNK * (q + 1)].rearrange(
-                        "(t p) j -> p t j", p=P
-                    ),
+                    out=x_rows[c][:, size * i : size * (i + 1), :],
+                    in_=rows[:, size * i : size * (i + 1), :],
                 )
+
+        def load_a(q, c):
+            a_piece[q, c] = raw.tile([P, PACK, CHUNK], BF16, name="raw_rows")
+            nc.sync.dma_start(
+                out=a_piece[q, c][:],
+                in_=A[CHUNK * c : CHUNK * (c + 1), CHUNK * q : CHUNK * (q + 1)].rearrange(
+                    "(t p) j -> p t j", p=P
+                ),
+            )
 
         w_scales = keep.tile([P, FEAT], U8, align_bytes=64)
         w_codes = keep.tile([P, FEAT], U32, align_bytes=64)
-        nc.vector.memset(w_scales[:].bitcast(I32), 0)
         bias_row = keep.tile([P, FEAT], BF16)
         nc.vector.memset(bias_row[:], 0.0)
+        nc.vector.memset(w_scales[:].bitcast(I32), 0)
         nc.scalar.dma_start(out=bias_row[0:1, :], in_=b1.unsqueeze(0))
 
         def load_w():
@@ -81,13 +102,15 @@ def tile_gcnnodeclassifiernetwork_pa_kernel(tc, A, x, W1_words, W1_scales, b1, o
                 in_=W1_words[0].rearrange("p n t -> p (n t)").bitcast(I32),
             )
 
-        load_x(0)
         for q in range(CHUNKS):
-            if q + 1 < CHUNKS:
-                load_x(q + 1)
-            load_a(q)
-            if q == 0:
-                load_w()
+            if q:
+                load_x(q, 1)
+            for c in range(CHUNKS):
+                if (q, c) == (0, 3):
+                    load_w()
+                load_a(q, c)
+                if (q, c) == (0, 0):
+                    load_x(0, 1)
 
         warm = keep.tile([P, 1], F32)
         nc.vector.memset(warm[:], 1.0)
@@ -96,7 +119,7 @@ def tile_gcnnodeclassifiernetwork_pa_kernel(tc, A, x, W1_words, W1_scales, b1, o
         make_identity(nc, ident[:])
         ones = keep.tile([P, P], BF16)
         nc.vector.memset(ones[:], 1.0)
-        bias_ps = psum.tile([P, FEAT], F32, tag="bank")
+        bias_ps = bank(SUMS_BANK, [P, FEAT])
         nc.tensor.matmul(out=bias_ps[:], lhsT=ones[:], rhs=bias_row[:], start=True, stop=True)
         bias = keep.tile([P, FEAT], F32)
         nc.scalar.copy(out=bias[:], in_=bias_ps[:])
@@ -107,16 +130,18 @@ def tile_gcnnodeclassifiernetwork_pa_kernel(tc, A, x, W1_words, W1_scales, b1, o
         a_scales = keep.tile([P, CHUNKS, NODES], U8, align_bytes=64)
         m_codes = keep.tile([P, CHUNKS, FEAT], U32, align_bytes=64)
         m_scales = keep.tile([P, CHUNKS, FEAT], U8, align_bytes=64)
-        self_loop = keep.tile([P, CHUNKS * PACK, FEAT], F32)
+        self_loop = keep.tile([P, BLOCKS, FEAT], F32)
+        sums_ps = {}
         d_of_chunk = {}
-        a_waiting = []
+        pieces = [(q, c) for q in range(CHUNKS) for c in range(CHUNKS)]
+        laid_out = []
 
         def quantise_x(c):
             words = x_rows[c][:].rearrange("p t k -> p (t k)").bitcast(F32)
             grouped = x_grouped.tile([P, PACK * P * PACK], BF16, align_bytes=64, name="x_side")
             grouped_words = grouped[:].bitcast(F32).rearrange("p (t r u) -> p t r u", t=PACK, u=2)
             for half in range(2):
-                flipped = psum.tile([P, 2, 2, P], F32, tag="bank")
+                flipped = scratch_bank([P, 2, 2, P])
                 for a in range(2):
                     first = (FEAT // 2) * (2 * half + a)
                     for u in range(2):
@@ -125,7 +150,8 @@ def tile_gcnnodeclassifiernetwork_pa_kernel(tc, A, x, W1_words, W1_scales, b1, o
                             in_=words[:, first + u : first + FEAT // 2 : 2],
                             identity=ident[:],
                         )
-                nc.scalar.copy(
+                copy = nc.vector.tensor_copy if c < 1 and half == 1 else nc.scalar.copy
+                copy(
                     out=grouped_words[:, 2 * half : 2 * half + 2, :, :],
                     in_=flipped[:].rearrange("p a u r -> p a r u"),
                 )
@@ -134,22 +160,33 @@ def tile_gcnnodeclassifiernetwork_pa_kernel(tc, A, x, W1_words, W1_scales, b1, o
                 out=x_codes[:, cols].bitcast(FP8X4), scales=x_scales[:, cols], in_=grouped[:]
             )
 
-        def column_sums(q):
-            sums_ps = psum.tile([P, PACK], F32, tag="bank")
+        def column_sums(q, c):
+            if c == 0:
+                sums_ps[q] = bank(SUMS_BANK, [P, PACK, CHUNKS])
             for b in range(PACK):
-                for c in range(CHUNKS):
-                    for t in range(PACK):
-                        nc.tensor.matmul(
-                            out=sums_ps[:, b : b + 1],
-                            lhsT=a_piece[q, c][:, t, P * b : P * (b + 1)],
-                            rhs=ones[:, 0:1],
-                            start=(c == 0 and t == 0),
-                            stop=(c == CHUNKS - 1 and t == PACK - 1),
-                        )
-            return sums_ps
+                for t in range(PACK):
+                    nc.tensor.matmul(
+                        out=sums_ps[q][:, b, c : c + 1],
+                        lhsT=a_piece[q, c][:, t, P * b : P * (b + 1)],
+                        rhs=ones[:, 0:1],
+                        start=(t == 0),
+                        stop=(t == PACK - 1),
+                    )
 
-        def quantise_waiting():
-            q, c, grouped = a_waiting.pop(0)
+        def lay_out(vector_cols):
+            q, c = pieces.pop(0)
+            piece = a_piece[q, c]
+            grouped = a_grouped.tile([P, CHUNK, PACK], BF16, align_bytes=64, name="a_side")
+            if vector_cols:
+                dst, src = side_by_side(grouped[:, :vector_cols, :], piece[:, :, :vector_cols])
+                nc.vector.tensor_copy(out=dst, in_=src)
+            if vector_cols < CHUNK:
+                dst, src = side_by_side(grouped[:, vector_cols:, :], piece[:, :, vector_cols:])
+                nc.scalar.copy(out=dst, in_=src)
+            laid_out.append((q, c, grouped))
+
+        def quantise_a():
+            q, c, grouped = laid_out.pop(0)
             cols = slice(CHUNK * q, CHUNK * (q + 1))
             nc.vector.quantize_mx(
                 out=a_codes[:, c, cols].bitcast(FP8X4),
@@ -157,23 +194,11 @@ def tile_gcnnodeclassifiernetwork_pa_kernel(tc, A, x, W1_words, W1_scales, b1, o
                 in_=grouped[:].rearrange("p j t -> p (j t)"),
             )
 
-        def quantise_a(q, c, vector_cols):
-            piece = a_piece[q, c]
-            grouped = a_grouped.tile([P, CHUNK, PACK], BF16, align_bytes=64, name="a_side")
-            if vector_cols:
-                dst, src = side_by_side(grouped[:, :vector_cols, :], piece[:, :, :vector_cols])
-                nc.vector.tensor_copy(out=dst, in_=src)
-            dst, src = side_by_side(grouped[:, vector_cols:, :], piece[:, :, vector_cols:])
-            nc.scalar.copy(out=dst, in_=src)
-            if a_waiting:
-                quantise_waiting()
-            a_waiting.append((q, c, grouped))
-
         def hidden(c):
             h_ps = []
             for t in range(PACK):
                 cols = slice(CHUNK * c + P * t, CHUNK * c + P * (t + 1))
-                h_ps.append(psum.tile([P, FEAT], F32, tag="bank", name="h_ps"))
+                h_ps.append(bank(HIDDEN_BANKS[t], [P, FEAT]))
                 nc.tensor.matmul_mx(
                     out=h_ps[t][:],
                     lhsT=x_codes[:, cols].bitcast(FP8X4),
@@ -185,21 +210,34 @@ def tile_gcnnodeclassifiernetwork_pa_kernel(tc, A, x, W1_words, W1_scales, b1, o
                 )
             return h_ps
 
-        def normalisers(sums_ps):
+        def normalisers(q):
+            column_sum = degrees.tile([P, PACK], F32)
+            four_sums = degrees.tile([P, PACK, CHUNKS], F32)
+            for b in range(PACK):
+                nc.scalar.activation(
+                    out=four_sums[:, b, :],
+                    in_=sums_ps[q][:, b, :],
+                    func=ACT.Copy,
+                    accum_out=column_sum[:, b : b + 1],
+                )
             d = degrees.tile([P, PACK], F32)
             nc.scalar.activation(
-                out=d[:], in_=sums_ps[:], func=ACT.Abs_reciprocal_sqrt, bias=1.0, scale=1.0
+                out=d[:], in_=column_sum[:], func=ACT.Abs_reciprocal_sqrt, bias=1.0, scale=1.0
             )
             d_squared = degrees.tile([P, PACK], F32)
             nc.scalar.activation(out=d_squared[:], in_=d[:], func=ACT.Square)
             return d, d_squared
 
-        def messages(c, h_ps, d, d_squared):
-            scaled = m_stage.tile([P, PACK, FEAT], BF16)
+        def scale_messages(h_ps, d):
+            scaled = m_stage.tile([P, PACK, FEAT], BF16, name="m_rows")
             for t in range(PACK):
                 nc.scalar.activation(
                     out=scaled[:, t, :], in_=h_ps[t][:], func=ACT.Copy, scale=d[:, t : t + 1]
                 )
+            return scaled
+
+        def self_loops(c, h_ps, d_squared):
+            for t in range(PACK):
                 nc.vector.scalar_tensor_tensor(
                     out=self_loop[:, PACK * c + t, :],
                     in0=h_ps[t][:],
@@ -208,28 +246,18 @@ def tile_gcnnodeclassifiernetwork_pa_kernel(tc, A, x, W1_words, W1_scales, b1, o
                     op0=ALU.mult,
                     op1=ALU.add,
                 )
+
+        def quantise_m(c, scaled):
             grouped = m_stage.tile([P, FEAT, PACK], BF16, align_bytes=64, name="m_side")
             dst, src = side_by_side(grouped[:], scaled[:])
             nc.vector.tensor_copy(out=dst, in_=src)
+            if laid_out:
+                quantise_a()
             nc.vector.quantize_mx(
                 out=m_codes[:, c, :].bitcast(FP8X4),
                 scales=m_scales[:, c, :],
                 in_=grouped[:].rearrange("p n t -> p (n t)"),
             )
-
-        last = CHUNKS - 1
-        quantise_x(0)
-        for q in range(CHUNKS):
-            if q < last:
-                quantise_x(q + 1)
-                for c in range(CHUNKS):
-                    quantise_a(q, c, VECTOR_COLS)
-            sums_ps = column_sums(q)
-            h_ps = hidden(q)
-            d_of_chunk[q], d_squared = normalisers(sums_ps)
-            messages(q, h_ps, d_of_chunk[q], d_squared)
-        for c in range(CHUNKS):
-            quantise_a(last, c, 0)
 
         agg_ps = {}
 
@@ -237,7 +265,7 @@ def tile_gcnnodeclassifiernetwork_pa_kernel(tc, A, x, W1_words, W1_scales, b1, o
             cols = slice(P * b, P * (b + 1))
             for c in which:
                 if c == 0:
-                    agg_ps[b] = psum.tile([P, FEAT], F32, tag="bank", name="agg_ps")
+                    agg_ps[b] = bank(AGG_BANKS[b % len(AGG_BANKS)], [P, FEAT])
                 nc.tensor.matmul_mx(
                     out=agg_ps[b][:],
                     lhsT=a_codes[:, c, cols].bitcast(FP8X4),
@@ -245,7 +273,7 @@ def tile_gcnnodeclassifiernetwork_pa_kernel(tc, A, x, W1_words, W1_scales, b1, o
                     rhs=m_codes[:, c, :].bitcast(FP8X4),
                     rhs_scale=m_scales[:, c, :],
                     start=(c == 0),
-                    stop=(c == last),
+                    stop=(c == LAST),
                 )
 
         def finish(b):
@@ -261,12 +289,34 @@ def tile_gcnnodeclassifiernetwork_pa_kernel(tc, A, x, W1_words, W1_scales, b1, o
             nc.scalar.activation(out=rows[:], in_=rows[:], func=ACT.Relu)
             nc.sync.dma_start(out=out[P * b : P * (b + 1), :], in_=rows[:])
 
-        for b in range(PSUM_BANKS):
-            passes(b, range(last))
-        for b in range(PSUM_BANKS):
-            passes(b, [last])
+        for q in range(CHUNKS):
+            for k in range(max(CHUNKS, PIECES_BEFORE_M[q])):
+                if k == X_AT[q]:
+                    quantise_x(q)
+                if k < CHUNKS:
+                    column_sums(q, k)
+                if k < PIECES_BEFORE_M[q]:
+                    lay_out(VECTOR_COLS[q])
+                    if len(laid_out) > 1:
+                        quantise_a()
+            h_ps = hidden(q)
+            d_of_chunk[q], d_squared = normalisers(q)
+            scaled = scale_messages(h_ps, d_of_chunk[q])
+            if q == LAST:
+                for b in range(PACK):
+                    passes(b, range(LAST))
+            self_loops(q, h_ps, d_squared)
+            quantise_m(q, scaled)
+
+        late = len(pieces)
+        for k in range(UP):
+            lay_out(VECTOR_COLS[-1])
+        for b in range(PACK, PACK + EXTRA):
+            passes(b, range(LAST))
+        for b in range(BLOCKS):
+            passes(b, [LAST] if b < PACK + EXTRA else range(CHUNKS))
             finish(b)
-        quantise_waiting()
-        for b in range(PSUM_BANKS, CHUNKS * PACK):
-            passes(b, range(CHUNKS))
-            finish(b)
+            if pieces:
+                lay_out(VECTOR_COLS[-1])
+            while laid_out and late - len(laid_out) - len(pieces) < late * (b + 1) // SPREAD:
+                quantise_a()

@@ -19,15 +19,13 @@ CHUNKS = NODES // CHUNK
 BLOCKS = NODES // P
 LAST = CHUNKS - 1
 HIDDEN_BANKS = (0, 1, 2, 3)
-SUMS_BANK = 4
-SCRATCH_BANKS = (5, 6, 7)
-AGG_BANKS = (5, 6, 7, 4, 0, 1, 2, 3)
-PIECES_BEFORE_M = (4, 3, 2, 1)
-VECTOR_COLS = (240, 208, 208, 208, 128)
-UP = 3
-SPREAD = 8
-EXTRA = 2
-X_AT = (1, 0, 0, 0)
+SUMS_BANKS = (4, 5, 6, 7)
+AGG_BANKS = (4, 5, 6, 7, 0, 1, 2, 3)
+PIECES_BEFORE_M = (4, 2, 2, 3)
+VECTOR_COLS = (208, 144, 144, 192, 128)
+UP = 5
+SPREAD = 7
+EXTRA = 3
 
 FLOPS = 2 * NODES * FEAT * FEAT + 2 * NODES * NODES * FEAT
 
@@ -55,12 +53,6 @@ def tile_gcnnodeclassifiernetwork_pa_kernel(tc, A, x, W1_words, W1_scales, b1, o
 
         def bank(i, shape, dtype=F32):
             return psum.tile(shape, dtype, tag="bank%d" % i, name="bank")
-
-        scratch_banks = list(SCRATCH_BANKS)
-
-        def scratch_bank(shape, dtype=F32):
-            scratch_banks.append(scratch_banks.pop(0))
-            return bank(scratch_banks[-1], shape, dtype)
 
         x_rows = {}
         a_piece = {}
@@ -103,14 +95,14 @@ def tile_gcnnodeclassifiernetwork_pa_kernel(tc, A, x, W1_words, W1_scales, b1, o
             )
 
         for q in range(CHUNKS):
-            if q:
-                load_x(q, 1)
             for c in range(CHUNKS):
                 if (q, c) == (0, 3):
                     load_w()
                 load_a(q, c)
                 if (q, c) == (0, 0):
                     load_x(0, 1)
+                if c == 3 and q < LAST:
+                    load_x(q + 1, 1)
 
         warm = keep.tile([P, 1], F32)
         nc.vector.memset(warm[:], 1.0)
@@ -119,7 +111,7 @@ def tile_gcnnodeclassifiernetwork_pa_kernel(tc, A, x, W1_words, W1_scales, b1, o
         make_identity(nc, ident[:])
         ones = keep.tile([P, P], BF16)
         nc.vector.memset(ones[:], 1.0)
-        bias_ps = bank(SUMS_BANK, [P, FEAT])
+        bias_ps = bank(SUMS_BANKS[0], [P, FEAT])
         nc.tensor.matmul(out=bias_ps[:], lhsT=ones[:], rhs=bias_row[:], start=True, stop=True)
         bias = keep.tile([P, FEAT], F32)
         nc.scalar.copy(out=bias[:], in_=bias_ps[:])
@@ -141,7 +133,7 @@ def tile_gcnnodeclassifiernetwork_pa_kernel(tc, A, x, W1_words, W1_scales, b1, o
             grouped = x_grouped.tile([P, PACK * P * PACK], BF16, align_bytes=64, name="x_side")
             grouped_words = grouped[:].bitcast(F32).rearrange("p (t r u) -> p t r u", t=PACK, u=2)
             for half in range(2):
-                flipped = scratch_bank([P, 2, 2, P])
+                flipped = bank(HIDDEN_BANKS[half], [P, 2, 2, P])
                 for a in range(2):
                     first = (FEAT // 2) * (2 * half + a)
                     for u in range(2):
@@ -162,15 +154,15 @@ def tile_gcnnodeclassifiernetwork_pa_kernel(tc, A, x, W1_words, W1_scales, b1, o
 
         def column_sums(q, c):
             if c == 0:
-                sums_ps[q] = bank(SUMS_BANK, [P, PACK, CHUNKS])
+                sums_ps[q] = [bank(i, [P, 1]) for i in SUMS_BANKS]
             for b in range(PACK):
                 for t in range(PACK):
                     nc.tensor.matmul(
-                        out=sums_ps[q][:, b, c : c + 1],
+                        out=sums_ps[q][b][:],
                         lhsT=a_piece[q, c][:, t, P * b : P * (b + 1)],
                         rhs=ones[:, 0:1],
-                        start=(t == 0),
-                        stop=(t == PACK - 1),
+                        start=(c == 0 and t == 0),
+                        stop=(c == LAST and t == PACK - 1),
                     )
 
         def lay_out(vector_cols):
@@ -211,30 +203,27 @@ def tile_gcnnodeclassifiernetwork_pa_kernel(tc, A, x, W1_words, W1_scales, b1, o
             return h_ps
 
         def normalisers(q):
-            column_sum = degrees.tile([P, PACK], F32)
-            four_sums = degrees.tile([P, PACK, CHUNKS], F32)
+            d = degrees.tile([P, PACK], F32)
             for b in range(PACK):
                 nc.scalar.activation(
-                    out=four_sums[:, b, :],
-                    in_=sums_ps[q][:, b, :],
-                    func=ACT.Copy,
-                    accum_out=column_sum[:, b : b + 1],
+                    out=d[:, b : b + 1],
+                    in_=sums_ps[q][b][:],
+                    func=ACT.Abs_reciprocal_sqrt,
+                    bias=1.0,
+                    scale=1.0,
                 )
-            d = degrees.tile([P, PACK], F32)
-            nc.scalar.activation(
-                out=d[:], in_=column_sum[:], func=ACT.Abs_reciprocal_sqrt, bias=1.0, scale=1.0
-            )
-            d_squared = degrees.tile([P, PACK], F32)
-            nc.scalar.activation(out=d_squared[:], in_=d[:], func=ACT.Square)
-            return d, d_squared
+            return d
 
         def scale_messages(h_ps, d):
             scaled = m_stage.tile([P, PACK, FEAT], BF16, name="m_rows")
+            d_squared = degrees.tile([P, PACK], F32)
             for t in range(PACK):
                 nc.scalar.activation(
                     out=scaled[:, t, :], in_=h_ps[t][:], func=ACT.Copy, scale=d[:, t : t + 1]
                 )
-            return scaled
+                if t == 0:
+                    nc.scalar.activation(out=d_squared[:], in_=d[:], func=ACT.Square)
+            return scaled, d_squared
 
         def self_loops(c, h_ps, d_squared):
             for t in range(PACK):
@@ -291,8 +280,8 @@ def tile_gcnnodeclassifiernetwork_pa_kernel(tc, A, x, W1_words, W1_scales, b1, o
 
         for q in range(CHUNKS):
             for k in range(max(CHUNKS, PIECES_BEFORE_M[q])):
-                if k == X_AT[q]:
-                    quantise_x(q)
+                if (q, k) == (0, 1):
+                    quantise_x(0)
                 if k < CHUNKS:
                     column_sums(q, k)
                 if k < PIECES_BEFORE_M[q]:
@@ -300,13 +289,15 @@ def tile_gcnnodeclassifiernetwork_pa_kernel(tc, A, x, W1_words, W1_scales, b1, o
                     if len(laid_out) > 1:
                         quantise_a()
             h_ps = hidden(q)
-            d_of_chunk[q], d_squared = normalisers(q)
-            scaled = scale_messages(h_ps, d_of_chunk[q])
+            d_of_chunk[q] = normalisers(q)
+            scaled, d_squared = scale_messages(h_ps, d_of_chunk[q])
             if q == LAST:
                 for b in range(PACK):
                     passes(b, range(LAST))
             self_loops(q, h_ps, d_squared)
             quantise_m(q, scaled)
+            if q < LAST:
+                quantise_x(q + 1)
 
         late = len(pieces)
         for k in range(UP):

@@ -32,8 +32,8 @@ FLOPS = 2 * NODES * FEAT * FEAT + 2 * NODES * NODES * FEAT
 
 def side_by_side(dst, src):
     return (
-        dst.rearrange("p (c i) t -> p c t i", i=4),
-        src.rearrange("p t (c i) -> p c t i", i=4),
+        dst.rearrange("p (c i) t -> p c t i", i=8),
+        src.rearrange("p t (c i) -> p c t i", i=8),
     )
 
 

@@ -19,13 +19,12 @@ CHUNKS = NODES // CHUNK
 BLOCKS = NODES // P
 LAST = CHUNKS - 1
 HIDDEN_BANKS = (0, 1, 2, 3)
-SUMS_BANKS = (4, 5, 6, 7)
-AGG_BANKS = (4, 5, 6, 7, 0, 1, 2, 3)
-PIECES_BEFORE_M = (4, 2, 2, 3)
-VECTOR_COLS = (208, 144, 144, 192, 128)
-UP = 5
-SPREAD = 7
-EXTRA = 3
+SUMS_BANK = 4
+AGG_BANKS = (5, 6, 7, 4, 0, 1, 2, 3)
+PSUM_BANKS = len(AGG_BANKS)
+PIECES_BEFORE_M = (4, 2, 2, 2)
+EARLY_VECTOR_COLS = 240
+LATE_VECTOR_COLS = 160
 
 FLOPS = 2 * NODES * FEAT * FEAT + 2 * NODES * NODES * FEAT
 
@@ -76,8 +75,8 @@ def tile_gcnnodeclassifiernetwork_pa_kernel(tc, A, x, W1_words, W1_scales, b1, o
                 ),
             )
 
-        w_scales = keep.tile([P, FEAT], U8, align_bytes=64)
-        w_codes = keep.tile([P, FEAT], U32, align_bytes=64)
+        w_scales = keep.tile([P, FEAT], U8, align_bytes=256)
+        w_codes = keep.tile([P, FEAT], U32, align_bytes=256)
         bias_row = keep.tile([P, FEAT], BF16)
         nc.vector.memset(bias_row[:], 0.0)
         nc.vector.memset(w_scales[:].bitcast(I32), 0)
@@ -111,17 +110,17 @@ def tile_gcnnodeclassifiernetwork_pa_kernel(tc, A, x, W1_words, W1_scales, b1, o
         make_identity(nc, ident[:])
         ones = keep.tile([P, P], BF16)
         nc.vector.memset(ones[:], 1.0)
-        bias_ps = bank(SUMS_BANKS[0], [P, FEAT])
+        bias_ps = bank(SUMS_BANK, [P, FEAT])
         nc.tensor.matmul(out=bias_ps[:], lhsT=ones[:], rhs=bias_row[:], start=True, stop=True)
         bias = keep.tile([P, FEAT], F32)
         nc.scalar.copy(out=bias[:], in_=bias_ps[:])
 
-        x_codes = keep.tile([P, NODES], U32, align_bytes=64)
-        x_scales = keep.tile([P, NODES], U8, align_bytes=64)
-        a_codes = keep.tile([P, CHUNKS, NODES], U32, align_bytes=64)
-        a_scales = keep.tile([P, CHUNKS, NODES], U8, align_bytes=64)
-        m_codes = keep.tile([P, CHUNKS, FEAT], U32, align_bytes=64)
-        m_scales = keep.tile([P, CHUNKS, FEAT], U8, align_bytes=64)
+        x_codes = keep.tile([P, NODES], U32, align_bytes=256)
+        x_scales = keep.tile([P, NODES], U8, align_bytes=256)
+        a_codes = keep.tile([P, CHUNKS, NODES], U32, align_bytes=256)
+        a_scales = keep.tile([P, CHUNKS, NODES], U8, align_bytes=256)
+        m_codes = keep.tile([P, CHUNKS, FEAT], U32, align_bytes=256)
+        m_scales = keep.tile([P, CHUNKS, FEAT], U8, align_bytes=256)
         self_loop = keep.tile([P, BLOCKS, FEAT], F32)
         sums_ps = {}
         d_of_chunk = {}
@@ -130,7 +129,7 @@ def tile_gcnnodeclassifiernetwork_pa_kernel(tc, A, x, W1_words, W1_scales, b1, o
 
         def quantise_x(c):
             words = x_rows[c][:].rearrange("p t k -> p (t k)").bitcast(F32)
-            grouped = x_grouped.tile([P, PACK * P * PACK], BF16, align_bytes=64, name="x_side")
+            grouped = x_grouped.tile([P, PACK * P * PACK], BF16, align_bytes=256, name="x_side")
             grouped_words = grouped[:].bitcast(F32).rearrange("p (t r u) -> p t r u", t=PACK, u=2)
             for half in range(2):
                 flipped = bank(HIDDEN_BANKS[half], [P, 2, 2, P])
@@ -152,23 +151,25 @@ def tile_gcnnodeclassifiernetwork_pa_kernel(tc, A, x, W1_words, W1_scales, b1, o
                 out=x_codes[:, cols].bitcast(FP8X4), scales=x_scales[:, cols], in_=grouped[:]
             )
 
-        def column_sums(q, c):
-            if c == 0:
-                sums_ps[q] = [bank(i, [P, 1]) for i in SUMS_BANKS]
+        def column_sums(q, pieces_of_part):
+            part = 0 if pieces_of_part[0] == 0 else 1
+            if part == 0:
+                sums_ps[q] = bank(SUMS_BANK, [P, 2, PACK])
             for b in range(PACK):
-                for t in range(PACK):
-                    nc.tensor.matmul(
-                        out=sums_ps[q][b][:],
-                        lhsT=a_piece[q, c][:, t, P * b : P * (b + 1)],
-                        rhs=ones[:, 0:1],
-                        start=(c == 0 and t == 0),
-                        stop=(c == LAST and t == PACK - 1),
-                    )
+                for c in pieces_of_part:
+                    for t in range(PACK):
+                        nc.tensor.matmul(
+                            out=sums_ps[q][:, part, b : b + 1],
+                            lhsT=a_piece[q, c][:, t, P * b : P * (b + 1)],
+                            rhs=ones[:, 0:1],
+                            start=(c == pieces_of_part[0] and t == 0),
+                            stop=(c == pieces_of_part[-1] and t == PACK - 1),
+                        )
 
         def lay_out(vector_cols):
             q, c = pieces.pop(0)
             piece = a_piece[q, c]
-            grouped = a_grouped.tile([P, CHUNK, PACK], BF16, align_bytes=64, name="a_side")
+            grouped = a_grouped.tile([P, CHUNK, PACK], BF16, align_bytes=256, name="a_side")
             if vector_cols:
                 dst, src = side_by_side(grouped[:, :vector_cols, :], piece[:, :, :vector_cols])
                 nc.vector.tensor_copy(out=dst, in_=src)
@@ -203,13 +204,17 @@ def tile_gcnnodeclassifiernetwork_pa_kernel(tc, A, x, W1_words, W1_scales, b1, o
             return h_ps
 
         def normalisers(q):
+            base = degrees.tile([P, PACK], F32)
+            nc.scalar.activation(
+                out=base[:], in_=sums_ps[q][:, 0, :], func=ACT.Identity, bias=1.0, scale=1.0
+            )
             d = degrees.tile([P, PACK], F32)
             for b in range(PACK):
                 nc.scalar.activation(
                     out=d[:, b : b + 1],
-                    in_=sums_ps[q][b][:],
+                    in_=sums_ps[q][:, 1, b : b + 1],
                     func=ACT.Abs_reciprocal_sqrt,
-                    bias=1.0,
+                    bias=base[:, b : b + 1],
                     scale=1.0,
                 )
             return d
@@ -237,7 +242,7 @@ def tile_gcnnodeclassifiernetwork_pa_kernel(tc, A, x, W1_words, W1_scales, b1, o
                 )
 
         def quantise_m(c, scaled):
-            grouped = m_stage.tile([P, FEAT, PACK], BF16, align_bytes=64, name="m_side")
+            grouped = m_stage.tile([P, FEAT, PACK], BF16, align_bytes=256, name="m_side")
             dst, src = side_by_side(grouped[:], scaled[:])
             nc.vector.tensor_copy(out=dst, in_=src)
             if laid_out:
@@ -279,35 +284,36 @@ def tile_gcnnodeclassifiernetwork_pa_kernel(tc, A, x, W1_words, W1_scales, b1, o
             nc.sync.dma_start(out=out[P * b : P * (b + 1), :], in_=rows[:])
 
         for q in range(CHUNKS):
-            for k in range(max(CHUNKS, PIECES_BEFORE_M[q])):
+            for k in range(CHUNKS):
                 if (q, k) == (0, 1):
                     quantise_x(0)
-                if k < CHUNKS:
-                    column_sums(q, k)
+                if k == LAST - 1:
+                    column_sums(q, range(LAST))
+                if k == LAST:
+                    column_sums(q, [LAST])
                 if k < PIECES_BEFORE_M[q]:
-                    lay_out(VECTOR_COLS[q])
+                    lay_out(EARLY_VECTOR_COLS)
                     if len(laid_out) > 1:
                         quantise_a()
             h_ps = hidden(q)
             d_of_chunk[q] = normalisers(q)
             scaled, d_squared = scale_messages(h_ps, d_of_chunk[q])
+            if q:
+                for b in range(PACK - 1):
+                    passes(b, [q - 1])
             if q == LAST:
-                for b in range(PACK):
-                    passes(b, range(LAST))
+                passes(PACK - 1, range(LAST))
             self_loops(q, h_ps, d_squared)
             quantise_m(q, scaled)
             if q < LAST:
                 quantise_x(q + 1)
 
-        late = len(pieces)
-        for k in range(UP):
-            lay_out(VECTOR_COLS[-1])
-        for b in range(PACK, PACK + EXTRA):
+        while pieces:
+            lay_out(LATE_VECTOR_COLS)
+        for b in range(PACK, PSUM_BANKS):
             passes(b, range(LAST))
         for b in range(BLOCKS):
-            passes(b, [LAST] if b < PACK + EXTRA else range(CHUNKS))
+            passes(b, [LAST] if b < PSUM_BANKS else range(CHUNKS))
             finish(b)
-            if pieces:
-                lay_out(VECTOR_COLS[-1])
-            while laid_out and late - len(laid_out) - len(pieces) < late * (b + 1) // SPREAD:
+            if laid_out:
                 quantise_a()

@@ -20,6 +20,7 @@ BLOCKS = NODES // P
 LAST = CHUNKS - 1
 HIDDEN_BANKS = (0, 1, 2, 3)
 SUMS_BANK = 4
+SUM_COLS = 48
 AGG_BANKS = (5, 6, 7, 4, 0, 1, 2, 3)
 PSUM_BANKS = len(AGG_BANKS)
 PIECES_BEFORE_M = (4, 2, 2, 2)
@@ -154,14 +155,14 @@ def tile_gcnnodeclassifiernetwork_pa_kernel(tc, A, x, W1_words, W1_scales, b1, o
         def column_sums(q, pieces_of_part):
             part = 0 if pieces_of_part[0] == 0 else 1
             if part == 0:
-                sums_ps[q] = bank(SUMS_BANK, [P, 2, PACK])
+                sums_ps[q] = bank(SUMS_BANK, [P, 2, PACK, SUM_COLS])
             for b in range(PACK):
                 for c in pieces_of_part:
                     for t in range(PACK):
                         nc.tensor.matmul(
-                            out=sums_ps[q][:, part, b : b + 1],
+                            out=sums_ps[q][:, part, b, :],
                             lhsT=a_piece[q, c][:, t, P * b : P * (b + 1)],
-                            rhs=ones[:, 0:1],
+                            rhs=ones[:, :SUM_COLS],
                             start=(c == pieces_of_part[0] and t == 0),
                             stop=(c == pieces_of_part[-1] and t == PACK - 1),
                         )
@@ -206,13 +207,13 @@ def tile_gcnnodeclassifiernetwork_pa_kernel(tc, A, x, W1_words, W1_scales, b1, o
         def normalisers(q):
             base = degrees.tile([P, PACK], F32)
             nc.scalar.activation(
-                out=base[:], in_=sums_ps[q][:, 0, :], func=ACT.Identity, bias=1.0, scale=1.0
+                out=base[:], in_=sums_ps[q][:, 0, :, 0], func=ACT.Identity, bias=1.0, scale=1.0
             )
             d = degrees.tile([P, PACK], F32)
             for b in range(PACK):
                 nc.scalar.activation(
                     out=d[:, b : b + 1],
-                    in_=sums_ps[q][:, 1, b : b + 1],
+                    in_=sums_ps[q][:, 1, b, 0:1],
                     func=ACT.Abs_reciprocal_sqrt,
                     bias=base[:, b : b + 1],
                     scale=1.0,

import concourse.mybir as mybir
from concourse.masks import make_identity

F32 = mybir.dt.float32
BF16 = mybir.dt.bfloat16
I32 = mybir.dt.int32
U32 = mybir.dt.uint32
U8 = mybir.dt.uint8
FP8X4 = mybir.dt.float8_e4m3fn_x4
ALU = mybir.AluOpType
ACT = mybir.ActivationFunctionType

P = 128
PACK = 4
CHUNK = P * PACK
NODES = 2048
FEAT = 512
CHUNKS = NODES // CHUNK
BLOCKS = NODES // P
LAST = CHUNKS - 1
HIDDEN_BANKS = (0, 1, 2, 3)
SUMS_BANK = 4
SUM_COLS = 48
AGG_BANKS = (5, 6, 7, 4, 0, 1, 2, 3)
PSUM_BANKS = len(AGG_BANKS)
PIECES_BEFORE_M = (4, 2, 2, 2)
EARLY_VECTOR_COLS = 240
LATE_VECTOR_COLS = 160

FLOPS = 2 * NODES * FEAT * FEAT + 2 * NODES * NODES * FEAT


def side_by_side(dst, src):
    return (
        dst.rearrange("p (c i) t -> p c t i", i=8),
        src.rearrange("p t (c i) -> p c t i", i=8),
    )


def tile_gcnnodeclassifiernetwork_pa_kernel(tc, A, x, W1_words, W1_scales, b1, out):
    nc = tc.nc
    with (
        tc.tile_pool(name="keep", bufs=1) as keep,
        tc.tile_pool(name="raw", bufs=16) as raw,
        tc.tile_pool(name="x_grouped", bufs=2) as x_grouped,
        tc.tile_pool(name="a_grouped", bufs=6) as a_grouped,
        tc.tile_pool(name="m_stage", bufs=2) as m_stage,
        tc.tile_pool(name="degrees", bufs=CHUNKS) as degrees,
        tc.tile_pool(name="result", bufs=8) as result,
        tc.psum_pool(name="psum", bufs=1) as psum,
        tc.manual_schedule(),
    ):

        def bank(i, shape, dtype=F32):
            return psum.tile(shape, dtype, tag="bank%d" % i, name="bank")

        x_rows = {}
        a_piece = {}

        def load_x(c, parts):
            x_rows[c] = raw.tile([P, PACK, FEAT], BF16, name="raw_rows")
            rows = x[CHUNK * c : CHUNK * (c + 1), :].rearrange("(t p) k -> p t k", p=P)
            size = PACK // parts
            for i in range(parts):
                nc.sync.dma_start(
                    out=x_rows[c][:, size * i : size * (i + 1), :],
                    in_=rows[:, size * i : size * (i + 1), :],
                )

        def load_a(q, c):
            a_piece[q, c] = raw.tile([P, PACK, CHUNK], BF16, name="raw_rows")
            nc.sync.dma_start(
                out=a_piece[q, c][:],
                in_=A[CHUNK * c : CHUNK * (c + 1), CHUNK * q : CHUNK * (q + 1)].rearrange(
                    "(t p) j -> p t j", p=P
                ),
            )

        w_scales = keep.tile([P, FEAT], U8, align_bytes=256)
        w_codes = keep.tile([P, FEAT], U32, align_bytes=256)
        bias_row = keep.tile([P, FEAT], BF16)
        nc.vector.memset(bias_row[:], 0.0)
        nc.vector.memset(w_scales[:].bitcast(I32), 0)
        nc.scalar.dma_start(out=bias_row[0:1, :], in_=b1.unsqueeze(0))

        def load_w():
            for quad in range(4):
                nc.sync.dma_start(
                    out=w_scales[32 * quad : 32 * quad + 4, :].bitcast(I32),
                    in_=W1_scales[0, 4 * quad : 4 * quad + 4, :].bitcast(I32),
                )
            nc.sync.dma_start(
                out=w_codes[:].bitcast(I32),
                in_=W1_words[0].rearrange("p n t -> p (n t)").bitcast(I32),
            )

        for q in range(CHUNKS):
            for c in range(CHUNKS):
                if (q, c) == (0, 3):
                    load_w()
                load_a(q, c)
                if (q, c) == (0, 0):
                    load_x(0, 1)
                if c == 3 and q < LAST:
                    load_x(q + 1, 1)

        warm = keep.tile([P, 1], F32)
        nc.vector.memset(warm[:], 1.0)
        nc.scalar.activation(out=warm[:], in_=warm[:], func=ACT.Abs_reciprocal_sqrt)
        ident = keep.tile([P, P], F32)
        make_identity(nc, ident[:])
        ones = keep.tile([P, P], BF16)
        nc.vector.memset(ones[:], 1.0)
        bias_ps = bank(SUMS_BANK, [P, FEAT])
        nc.tensor.matmul(out=bias_ps[:], lhsT=ones[:], rhs=bias_row[:], start=True, stop=True)
        bias = keep.tile([P, FEAT], F32)
        nc.scalar.copy(out=bias[:], in_=bias_ps[:])

        x_codes = keep.tile([P, NODES], U32, align_bytes=256)
        x_scales = keep.tile([P, NODES], U8, align_bytes=256)
        a_codes = keep.tile([P, CHUNKS, NODES], U32, align_bytes=256)
        a_scales = keep.tile([P, CHUNKS, NODES], U8, align_bytes=256)
        m_codes = keep.tile([P, CHUNKS, FEAT], U32, align_bytes=256)
        m_scales = keep.tile([P, CHUNKS, FEAT], U8, align_bytes=256)
        self_loop = keep.tile([P, BLOCKS, FEAT], F32)
        sums_ps = {}
        d_of_chunk = {}
        pieces = [(q, c) for q in range(CHUNKS) for c in range(CHUNKS)]
        laid_out = []

        def quantise_x(c):
            words = x_rows[c][:].rearrange("p t k -> p (t k)").bitcast(F32)
            grouped = x_grouped.tile([P, PACK * P * PACK], BF16, align_bytes=256, name="x_side")
            grouped_words = grouped[:].bitcast(F32).rearrange("p (t r u) -> p t r u", t=PACK, u=2)
            for half in range(2):
                flipped = bank(HIDDEN_BANKS[half], [P, 2, 2, P])
                for a in range(2):
                    first = (FEAT // 2) * (2 * half + a)
                    for u in range(2):
                        nc.tensor.transpose(
                            out=flipped[:, a, u, :],
                            in_=words[:, first + u : first + FEAT // 2 : 2],
                            identity=ident[:],
                        )
                copy = nc.vector.tensor_copy if c < 1 and half == 1 else nc.scalar.copy
                copy(
                    out=grouped_words[:, 2 * half : 2 * half + 2, :, :],
                    in_=flipped[:].rearrange("p a u r -> p a r u"),
                )
            cols = slice(CHUNK * c, CHUNK * (c + 1))
            nc.vector.quantize_mx(
                out=x_codes[:, cols].bitcast(FP8X4), scales=x_scales[:, cols], in_=grouped[:]
            )

        def column_sums(q, pieces_of_part):
            part = 0 if pieces_of_part[0] == 0 else 1
            if part == 0:
                sums_ps[q] = bank(SUMS_BANK, [P, 2, PACK, SUM_COLS])
            for b in range(PACK):
                for c in pieces_of_part:
                    for t in range(PACK):
                        nc.tensor.matmul(
                            out=sums_ps[q][:, part, b, :],
                            lhsT=a_piece[q, c][:, t, P * b : P * (b + 1)],
                            rhs=ones[:, :SUM_COLS],
                            start=(c == pieces_of_part[0] and t == 0),
                            stop=(c == pieces_of_part[-1] and t == PACK - 1),
                        )

        def lay_out(vector_cols):
            q, c = pieces.pop(0)
            piece = a_piece[q, c]
            grouped = a_grouped.tile([P, CHUNK, PACK], BF16, align_bytes=256, name="a_side")
            if vector_cols:
                dst, src = side_by_side(grouped[:, :vector_cols, :], piece[:, :, :vector_cols])
                nc.vector.tensor_copy(out=dst, in_=src)
            if vector_cols < CHUNK:
                dst, src = side_by_side(grouped[:, vector_cols:, :], piece[:, :, vector_cols:])
                nc.scalar.copy(out=dst, in_=src)
            laid_out.append((q, c, grouped))

        def quantise_a():
            q, c, grouped = laid_out.pop(0)
            cols = slice(CHUNK * q, CHUNK * (q + 1))
            nc.vector.quantize_mx(
                out=a_codes[:, c, cols].bitcast(FP8X4),
                scales=a_scales[:, c, cols],
                in_=grouped[:].rearrange("p j t -> p (j t)"),
            )

        def hidden(c):
            h_ps = []
            for t in range(PACK):
                cols = slice(CHUNK * c + P * t, CHUNK * c + P * (t + 1))
                h_ps.append(bank(HIDDEN_BANKS[t], [P, FEAT]))
                nc.tensor.matmul_mx(
                    out=h_ps[t][:],
                    lhsT=x_codes[:, cols].bitcast(FP8X4),
                    lhsT_scale=x_scales[:, cols],
                    rhs=w_codes[:].bitcast(FP8X4),
                    rhs_scale=w_scales[:],
                    start=True,
                    stop=True,
                )
            return h_ps

        def normalisers(q):
            base = degrees.tile([P, PACK], F32)
            nc.scalar.activation(
                out=base[:], in_=sums_ps[q][:, 0, :, 0], func=ACT.Identity, bias=1.0, scale=1.0
            )
            d = degrees.tile([P, PACK], F32)
            for b in range(PACK):
                nc.scalar.activation(
                    out=d[:, b : b + 1],
                    in_=sums_ps[q][:, 1, b, 0:1],
                    func=ACT.Abs_reciprocal_sqrt,
                    bias=base[:, b : b + 1],
                    scale=1.0,
                )
            return d

        def scale_messages(h_ps, d):
            scaled = m_stage.tile([P, PACK, FEAT], BF16, name="m_rows")
            d_squared = degrees.tile([P, PACK], F32)
            for t in range(PACK):
                nc.scalar.activation(
                    out=scaled[:, t, :], in_=h_ps[t][:], func=ACT.Copy, scale=d[:, t : t + 1]
                )
                if t == 0:
                    nc.scalar.activation(out=d_squared[:], in_=d[:], func=ACT.Square)
            return scaled, d_squared

        def self_loops(c, h_ps, d_squared):
            for t in range(PACK):
                nc.vector.scalar_tensor_tensor(
                    out=self_loop[:, PACK * c + t, :],
                    in0=h_ps[t][:],
                    scalar=d_squared[:, t : t + 1],
                    in1=bias[:],
                    op0=ALU.mult,
                    op1=ALU.add,
                )

        def quantise_m(c, scaled):
            grouped = m_stage.tile([P, FEAT, PACK], BF16, align_bytes=256, name="m_side")
            dst, src = side_by_side(grouped[:], scaled[:])
            nc.vector.tensor_copy(out=dst, in_=src)
            if laid_out:
                quantise_a()
            nc.vector.quantize_mx(
                out=m_codes[:, c, :].bitcast(FP8X4),
                scales=m_scales[:, c, :],
                in_=grouped[:].rearrange("p n t -> p (n t)"),
            )

        agg_ps = {}

        def passes(b, which):
            cols = slice(P * b, P * (b + 1))
            for c in which:
                if c == 0:
                    agg_ps[b] = bank(AGG_BANKS[b % len(AGG_BANKS)], [P, FEAT])
                nc.tensor.matmul_mx(
                    out=agg_ps[b][:],
                    lhsT=a_codes[:, c, cols].bitcast(FP8X4),
                    lhsT_scale=a_scales[:, c, cols],
                    rhs=m_codes[:, c, :].bitcast(FP8X4),
                    rhs_scale=m_scales[:, c, :],
                    start=(c == 0),
                    stop=(c == LAST),
                )

        def finish(b):
            rows = result.tile([P, FEAT], F32)
            nc.vector.scalar_tensor_tensor(
                out=rows[:],
                in0=agg_ps[b][:],
                scalar=d_of_chunk[b // PACK][:, b % PACK : b % PACK + 1],
                in1=self_loop[:, b, :],
                op0=ALU.mult,
                op1=ALU.add,
            )
            nc.scalar.activation(out=rows[:], in_=rows[:], func=ACT.Relu)
            nc.sync.dma_start(out=out[P * b : P * (b + 1), :], in_=rows[:])

        for q in range(CHUNKS):
            for k in range(CHUNKS):
                if (q, k) == (0, 1):
                    quantise_x(0)
                if k == LAST - 1:
                    column_sums(q, range(LAST))
                if k == LAST:
                    column_sums(q, [LAST])
                if k < PIECES_BEFORE_M[q]:
                    lay_out(EARLY_VECTOR_COLS)
                    if len(laid_out) > 1:
                        quantise_a()
            h_ps = hidden(q)
            d_of_chunk[q] = normalisers(q)
            scaled, d_squared = scale_messages(h_ps, d_of_chunk[q])
            if q:
                for b in range(PACK - 1):
                    passes(b, [q - 1])
            if q == LAST:
                passes(PACK - 1, range(LAST))
            self_loops(q, h_ps, d_squared)
            quantise_m(q, scaled)
            if q < LAST:
                quantise_x(q + 1)

        while pieces:
            lay_out(LATE_VECTOR_COLS)
        for b in range(PACK, PSUM_BANKS):
            passes(b, range(LAST))
        for b in range(BLOCKS):
            passes(b, [LAST] if b < PSUM_BANKS else range(CHUNKS))
            finish(b)
            if laid_out:
                quantise_a()
